import numpy as np
import ml_dtypes

BF16 = ml_dtypes.bfloat16


def bf(x):
    return np.asarray(x, np.float32).astype(BF16)


def f32(x):
    return np.asarray(x, np.float32)


def f64(x):
    return np.asarray(x).astype(np.float64)


def striped(idx):
    return np.tile(idx.reshape(-1, 16).T, (8, 1))


C, E, S, N, Q = 256, 128, 512, 128, 3


def sigmoid(v):
    return 1.0 / (1.0 + np.exp(-v))


def setup_inputs():
    return {
        "base": f32(0.5 * np.random.standard_normal((C, S))),
        "x": bf(np.random.standard_normal((E, N))),
        "w_ih": bf(np.random.standard_normal((E, Q * C)) / np.sqrt(E)),
        "b_ih": f32(0.5 * np.random.standard_normal((Q * C, 1))),
        "b_hh": f32(0.5 * np.random.standard_normal((Q * C, 1))),
        "offs": striped(np.random.permutation(S)[:N]),
    }


def reference(base, x, w_ih, b_ih, b_hh, offs):
    idx = offs[:16].T.reshape(-1)
    a = f64(w_ih).T @ f64(x) + f64(b_ih)
    i_r, i_z, i_n = a.reshape(Q, C, N)
    h_r, h_z, h_n = f64(b_hh).reshape(Q, C, 1)
    r = sigmoid(i_r + h_r)
    z = sigmoid(i_z + h_z)
    n = np.tanh(i_n + r * h_n)
    out = f64(base).copy()
    out[:, idx] = (1.0 - z) * n
    return out

@@ -1,0 +1,78 @@
+import concourse.mybir as mybir
+
+F32, BF16, U16 = mybir.dt.float32, mybir.dt.bfloat16, mybir.dt.uint16
+MULT, ADD, SUBTRACT = mybir.AluOpType.mult, mybir.AluOpType.add, mybir.AluOpType.subtract
+SIGMOID, TANH = mybir.ActivationFunctionType.Sigmoid, mybir.ActivationFunctionType.Tanh
+
+P = 128
+C, E, S, N = 256, 128, 512, 128
+BLOCKS = C // P
+R, Z, NEW = 0, 1, 2
+GATES = 3
+
+FLOPS = 2 * E * GATES * C * N
+
+
+def tile_batchtreeencoder_kernel(tc, base, x, w_ih, b_ih, b_hh, offs, out):
+    nc = tc.nc
+    with tc.tile_pool(name="held", bufs=1) as held, tc.psum_pool(name="psum", bufs=1) as psum:
+        offsets = held.tile([P, N // 16], U16, name="offsets")
+        nc.sync.dma_start(offsets[:], offs)
+        nodes = held.tile([E, N], BF16, name="nodes")
+        nc.sync.dma_start(nodes[:], x)
+        weights = held.tile([E, GATES * C], BF16, name="weights")
+        nc.sync.dma_start(weights[:], w_ih)
+        bias_ih = held.tile([P, GATES * BLOCKS], F32, name="bias_ih")
+        bias_hh = held.tile([P, GATES * BLOCKS], F32, name="bias_hh")
+        with nc.allow_non_contiguous_dma(reason="a bias goes one element to a partition"):
+            nc.scalar.dma_start(bias_ih[:], b_ih.rearrange("(k p) o -> p (k o)", p=P))
+            nc.scalar.dma_start(bias_hh[:], b_hh.rearrange("(k p) o -> p (k o)", p=P))
+        windows = [held.tile([P, S], F32, name=f"window{b}") for b in range(BLOCKS)]
+        nc.sync.dma_start(windows[0][:], base[0:P, :])
+        nc.scalar.dma_start(windows[1][:], base[P : 2 * P, :])
+
+        def column(gate, b):
+            return slice(gate * BLOCKS + b, gate * BLOCKS + b + 1)
+
+        bias_r = held.tile([P, BLOCKS], F32, name="bias_r")
+        nc.vector.tensor_tensor(
+            bias_r[:], bias_ih[:, R * BLOCKS : (R + 1) * BLOCKS], bias_hh[:, R * BLOCKS : (R + 1) * BLOCKS], ADD
+        )
+        minus_bias_z = held.tile([P, BLOCKS], F32, name="minus_bias_z")
+        nc.vector.scalar_tensor_tensor(
+            minus_bias_z[:],
+            bias_ih[:, Z * BLOCKS : (Z + 1) * BLOCKS],
+            -1.0,
+            bias_hh[:, Z * BLOCKS : (Z + 1) * BLOCKS],
+            MULT,
+            SUBTRACT,
+        )
+
+        products = {}
+        for gate in (R, NEW, Z):
+            for b in range(BLOCKS):
+                products[gate, b] = psum.tile([P, N], F32, name=f"product{gate}{b}")
+                first = gate * C + b * P
+                nc.tensor.matmul(products[gate, b][:], weights[:, first : first + P], nodes[:], start=True, stop=True)
+
+        reset = [held.tile([P, N], F32, name=f"reset{b}") for b in range(BLOCKS)]
+        for b in range(BLOCKS):
+            nc.scalar.activation(reset[b][:], products[R, b][:], SIGMOID, bias=bias_r[:, b : b + 1], scale=1.0)
+        before_tanh = [held.tile([P, N], F32, name=f"before_tanh{b}") for b in range(BLOCKS)]
+        for b in range(BLOCKS):
+            nc.vector.scalar_tensor_tensor(
+                before_tanh[b][:], reset[b][:], bias_hh[:, column(NEW, b)], products[NEW, b][:], MULT, ADD
+            )
+        one_minus_z = [held.tile([P, N], F32, name=f"one_minus_z{b}") for b in range(BLOCKS)]
+        for b in range(BLOCKS):
+            nc.scalar.activation(
+                one_minus_z[b][:], products[Z, b][:], SIGMOID, bias=minus_bias_z[:, b : b + 1], scale=-1.0
+            )
+        new = [held.tile([P, N], F32, name=f"new{b}") for b in range(BLOCKS)]
+        for b in range(BLOCKS):
+            nc.scalar.activation(new[b][:], before_tanh[b][:], TANH, bias=bias_ih[:, column(NEW, b)], scale=1.0)
+
+        for b in range(BLOCKS):
+            nc.vector.tensor_tensor(windows[b][:].indirect(offsets[:]), one_minus_z[b][:], new[b][:], MULT)
+        nc.sync.dma_start(out[0:P, :], windows[0][:])
+        nc.scalar.dma_start(out[P : 2 * P, :], windows[1][:])

@@ -31,6 +31,11 @@ def tile_batchtreeencoder_kernel(tc, base, x, w_ih, b_ih, b_hh, offs, out):
         nc.sync.dma_start(windows[0][:], base[0:P, :])
         nc.scalar.dma_start(windows[1][:], base[P : 2 * P, :])
 
+        zero = held.tile([P, 1], F32, name="zero")
+        nc.vector.memset(zero[:], 0.0)
+        warmed = held.tile([P, 1], F32, name="warmed")
+        nc.scalar.activation(warmed[:], zero[:], SIGMOID)
+
         def column(gate, b):
             return slice(gate * BLOCKS + b, gate * BLOCKS + b + 1)
 

@@ -1,3 +1,4 @@
+import concourse.masks as masks
 import concourse.mybir as mybir
 
 F32, BF16, U16 = mybir.dt.float32, mybir.dt.bfloat16, mybir.dt.uint16
@@ -9,6 +10,7 @@ C, E, S, N = 256, 128, 512, 128
 BLOCKS = C // P
 R, Z, NEW = 0, 1, 2
 GATES = 3
+PIECES = GATES * BLOCKS
 
 FLOPS = 2 * E * GATES * C * N
 
@@ -22,11 +24,9 @@ def tile_batchtreeencoder_kernel(tc, base, x, w_ih, b_ih, b_hh, offs, out):
         nc.sync.dma_start(nodes[:], x)
         weights = held.tile([E, GATES * C], BF16, name="weights")
         nc.sync.dma_start(weights[:], w_ih)
-        bias_ih = held.tile([P, GATES * BLOCKS], F32, name="bias_ih")
-        bias_hh = held.tile([P, GATES * BLOCKS], F32, name="bias_hh")
-        with nc.allow_non_contiguous_dma(reason="a bias goes one element to a partition"):
-            nc.scalar.dma_start(bias_ih[:], b_ih.rearrange("(k p) o -> p (k o)", p=P))
-            nc.scalar.dma_start(bias_hh[:], b_hh.rearrange("(k p) o -> p (k o)", p=P))
+        bias_rows = held.tile([2 * PIECES, P], F32, name="bias_rows")
+        nc.scalar.dma_start(bias_rows[0:PIECES, :], b_ih.rearrange("(k p) o -> k (p o)", p=P))
+        nc.scalar.dma_start(bias_rows[PIECES : 2 * PIECES, :], b_hh.rearrange("(k p) o -> k (p o)", p=P))
         windows = [held.tile([P, S], F32, name=f"window{b}") for b in range(BLOCKS)]
         nc.sync.dma_start(windows[0][:], base[0:P, :])
         nc.scalar.dma_start(windows[1][:], base[P : 2 * P, :])
@@ -35,6 +35,15 @@ def tile_batchtreeencoder_kernel(tc, base, x, w_ih, b_ih, b_hh, offs, out):
         nc.vector.memset(zero[:], 0.0)
         warmed = held.tile([P, 1], F32, name="warmed")
         nc.scalar.activation(warmed[:], zero[:], SIGMOID)
+
+        identity = held.tile([2 * PIECES, 2 * PIECES], F32, name="identity")
+        masks.make_identity(nc, identity[:])
+        bias_columns = psum.tile([P, 2 * PIECES], F32, name="bias_columns")
+        nc.tensor.matmul(bias_columns[:], bias_rows[:], identity[:], start=True, stop=True)
+        biases = held.tile([P, 2 * PIECES], F32, name="biases")
+        nc.vector.tensor_copy(biases[:], bias_columns[:])
+        bias_ih = biases[:, 0:PIECES]
+        bias_hh = biases[:, PIECES : 2 * PIECES]
 
         def column(gate, b):
             return slice(gate * BLOCKS + b, gate * BLOCKS + b + 1)

@@ -1,4 +1,3 @@
-import concourse.masks as masks
 import concourse.mybir as mybir
 
 F32, BF16, U16 = mybir.dt.float32, mybir.dt.bfloat16, mybir.dt.uint16
@@ -10,7 +9,7 @@ C, E, S, N = 256, 128, 512, 128
 BLOCKS = C // P
 R, Z, NEW = 0, 1, 2
 GATES = 3
-PIECES = GATES * BLOCKS
+STORES = 4
 
 FLOPS = 2 * E * GATES * C * N
 
@@ -24,9 +23,11 @@ def tile_batchtreeencoder_kernel(tc, base, x, w_ih, b_ih, b_hh, offs, out):
         nc.sync.dma_start(nodes[:], x)
         weights = held.tile([E, GATES * C], BF16, name="weights")
         nc.sync.dma_start(weights[:], w_ih)
-        bias_rows = held.tile([2 * PIECES, P], F32, name="bias_rows")
-        nc.scalar.dma_start(bias_rows[0:PIECES, :], b_ih.rearrange("(k p) o -> k (p o)", p=P))
-        nc.scalar.dma_start(bias_rows[PIECES : 2 * PIECES, :], b_hh.rearrange("(k p) o -> k (p o)", p=P))
+        bias_ih = held.tile([P, GATES * BLOCKS], F32, name="bias_ih")
+        bias_hh = held.tile([P, GATES * BLOCKS], F32, name="bias_hh")
+        with nc.allow_non_contiguous_dma(reason="a bias goes one element to a partition"):
+            nc.scalar.dma_start(bias_ih[:], b_ih.rearrange("(k p) o -> p (k o)", p=P))
+            nc.scalar.dma_start(bias_hh[:], b_hh.rearrange("(k p) o -> p (k o)", p=P))
         windows = [held.tile([P, S], F32, name=f"window{b}") for b in range(BLOCKS)]
         nc.sync.dma_start(windows[0][:], base[0:P, :])
         nc.scalar.dma_start(windows[1][:], base[P : 2 * P, :])
@@ -35,15 +36,6 @@ def tile_batchtreeencoder_kernel(tc, base, x, w_ih, b_ih, b_hh, offs, out):
         nc.vector.memset(zero[:], 0.0)
         warmed = held.tile([P, 1], F32, name="warmed")
         nc.scalar.activation(warmed[:], zero[:], SIGMOID)
-
-        identity = held.tile([2 * PIECES, 2 * PIECES], F32, name="identity")
-        masks.make_identity(nc, identity[:])
-        bias_columns = psum.tile([P, 2 * PIECES], F32, name="bias_columns")
-        nc.tensor.matmul(bias_columns[:], bias_rows[:], identity[:], start=True, stop=True)
-        biases = held.tile([P, 2 * PIECES], F32, name="biases")
-        nc.vector.tensor_copy(biases[:], bias_columns[:])
-        bias_ih = biases[:, 0:PIECES]
-        bias_hh = biases[:, PIECES : 2 * PIECES]
 
         def column(gate, b):
             return slice(gate * BLOCKS + b, gate * BLOCKS + b + 1)
@@ -86,7 +78,10 @@ def tile_batchtreeencoder_kernel(tc, base, x, w_ih, b_ih, b_hh, offs, out):
         for b in range(BLOCKS):
             nc.scalar.activation(new[b][:], before_tanh[b][:], TANH, bias=bias_ih[:, column(NEW, b)], scale=1.0)
 
+        width = S // STORES
         for b in range(BLOCKS):
             nc.vector.tensor_tensor(windows[b][:].indirect(offsets[:]), one_minus_z[b][:], new[b][:], MULT)
-        nc.sync.dma_start(out[0:P, :], windows[0][:])
-        nc.scalar.dma_start(out[P : 2 * P, :], windows[1][:])
+            for piece in range(STORES):
+                queue = nc.sync if piece % 2 == 0 else nc.scalar
+                columns = slice(piece * width, (piece + 1) * width)
+                queue.dma_start(out[b * P : (b + 1) * P, columns], windows[b][:, columns])

@@ -9,7 +9,7 @@ C, E, S, N = 256, 128, 512, 128
 BLOCKS = C // P
 R, Z, NEW = 0, 1, 2
 GATES = 3
-STORES = 4
+GATE_ORDER = (R, NEW, Z)
 
 FLOPS = 2 * E * GATES * C * N
 
@@ -17,20 +17,22 @@ FLOPS = 2 * E * GATES * C * N
 def tile_batchtreeencoder_kernel(tc, base, x, w_ih, b_ih, b_hh, offs, out):
     nc = tc.nc
     with tc.tile_pool(name="held", bufs=1) as held, tc.psum_pool(name="psum", bufs=1) as psum:
+        weights = {}
+        for gate in GATE_ORDER:
+            weights[gate] = held.tile([E, C], BF16, name=f"weights{gate}")
+            nc.sync.dma_start(weights[gate][:], w_ih[:, gate * C : (gate + 1) * C])
         offsets = held.tile([P, N // 16], U16, name="offsets")
         nc.sync.dma_start(offsets[:], offs)
+        windows = [held.tile([P, S], F32, name=f"window{b}") for b in range(BLOCKS)]
+        for b in range(BLOCKS):
+            nc.sync.dma_start(windows[b][:], base[b * P : (b + 1) * P, :])
         nodes = held.tile([E, N], BF16, name="nodes")
-        nc.sync.dma_start(nodes[:], x)
-        weights = held.tile([E, GATES * C], BF16, name="weights")
-        nc.sync.dma_start(weights[:], w_ih)
+        nc.scalar.dma_start(nodes[:], x)
         bias_ih = held.tile([P, GATES * BLOCKS], F32, name="bias_ih")
         bias_hh = held.tile([P, GATES * BLOCKS], F32, name="bias_hh")
         with nc.allow_non_contiguous_dma(reason="a bias goes one element to a partition"):
             nc.scalar.dma_start(bias_ih[:], b_ih.rearrange("(k p) o -> p (k o)", p=P))
             nc.scalar.dma_start(bias_hh[:], b_hh.rearrange("(k p) o -> p (k o)", p=P))
-        windows = [held.tile([P, S], F32, name=f"window{b}") for b in range(BLOCKS)]
-        nc.sync.dma_start(windows[0][:], base[0:P, :])
-        nc.scalar.dma_start(windows[1][:], base[P : 2 * P, :])
 
         zero = held.tile([P, 1], F32, name="zero")
         nc.vector.memset(zero[:], 0.0)
@@ -55,11 +57,12 @@ def tile_batchtreeencoder_kernel(tc, base, x, w_ih, b_ih, b_hh, offs, out):
         )
 
         products = {}
-        for gate in (R, NEW, Z):
+        for gate in GATE_ORDER:
             for b in range(BLOCKS):
                 products[gate, b] = psum.tile([P, N], F32, name=f"product{gate}{b}")
-                first = gate * C + b * P
-                nc.tensor.matmul(products[gate, b][:], weights[:, first : first + P], nodes[:], start=True, stop=True)
+                nc.tensor.matmul(
+                    products[gate, b][:], weights[gate][:, b * P : (b + 1) * P], nodes[:], start=True, stop=True
+                )
 
         reset = [held.tile([P, N], F32, name=f"reset{b}") for b in range(BLOCKS)]
         for b in range(BLOCKS):
@@ -78,10 +81,7 @@ def tile_batchtreeencoder_kernel(tc, base, x, w_ih, b_ih, b_hh, offs, out):
         for b in range(BLOCKS):
             nc.scalar.activation(new[b][:], before_tanh[b][:], TANH, bias=bias_ih[:, column(NEW, b)], scale=1.0)
 
-        width = S // STORES
         for b in range(BLOCKS):
             nc.vector.tensor_tensor(windows[b][:].indirect(offsets[:]), one_minus_z[b][:], new[b][:], MULT)
-            for piece in range(STORES):
-                queue = nc.sync if piece % 2 == 0 else nc.scalar
-                columns = slice(piece * width, (piece + 1) * width)
-                queue.dma_start(out[b * P : (b + 1) * P, columns], windows[b][:, columns])
+        nc.sync.dma_start(out[0:P, :], windows[0][:])
+        nc.scalar.dma_start(out[P : 2 * P, :], windows[1][:])

@@ -9,7 +9,6 @@ C, E, S, N = 256, 128, 512, 128
 BLOCKS = C // P
 R, Z, NEW = 0, 1, 2
 GATES = 3
-GATE_ORDER = (R, NEW, Z)
 
 FLOPS = 2 * E * GATES * C * N
 
@@ -17,22 +16,24 @@ FLOPS = 2 * E * GATES * C * N
 def tile_batchtreeencoder_kernel(tc, base, x, w_ih, b_ih, b_hh, offs, out):
     nc = tc.nc
     with tc.tile_pool(name="held", bufs=1) as held, tc.psum_pool(name="psum", bufs=1) as psum:
-        weights = {}
-        for gate in GATE_ORDER:
-            weights[gate] = held.tile([E, C], BF16, name=f"weights{gate}")
-            nc.sync.dma_start(weights[gate][:], w_ih[:, gate * C : (gate + 1) * C])
+        nodes = held.tile([E, N], BF16, name="nodes")
+        nc.sync.dma_start(nodes[:], x)
+        weights = held.tile([E, GATES * C], BF16, name="weights")
+        nc.sync.dma_start(weights[:], w_ih)
         offsets = held.tile([P, N // 16], U16, name="offsets")
         nc.sync.dma_start(offsets[:], offs)
-        windows = [held.tile([P, S], F32, name=f"window{b}") for b in range(BLOCKS)]
-        for b in range(BLOCKS):
-            nc.sync.dma_start(windows[b][:], base[b * P : (b + 1) * P, :])
-        nodes = held.tile([E, N], BF16, name="nodes")
-        nc.scalar.dma_start(nodes[:], x)
         bias_ih = held.tile([P, GATES * BLOCKS], F32, name="bias_ih")
         bias_hh = held.tile([P, GATES * BLOCKS], F32, name="bias_hh")
-        with nc.allow_non_contiguous_dma(reason="a bias goes one element to a partition"):
-            nc.scalar.dma_start(bias_ih[:], b_ih.rearrange("(k p) o -> p (k o)", p=P))
-            nc.scalar.dma_start(bias_hh[:], b_hh.rearrange("(k p) o -> p (k o)", p=P))
+        for tile, bias in ((bias_ih, b_ih), (bias_hh, b_hh)):
+            nc.scalar.dma_start(
+                tile[:].rearrange("p (g b) -> p g b", g=GATES),
+                bias.rearrange("(g p b) o -> p g (b o)", g=GATES, b=BLOCKS),
+            )
+        base_blocks = base.rearrange("(p b) s -> b p s", b=BLOCKS)
+        out_blocks = out.rearrange("(p b) s -> b p s", b=BLOCKS)
+        windows = [held.tile([P, S], F32, name=f"window{b}") for b in range(BLOCKS)]
+        nc.sync.dma_start(windows[0][:], base_blocks[0])
+        nc.scalar.dma_start(windows[1][:], base_blocks[1])
 
         zero = held.tile([P, 1], F32, name="zero")
         nc.vector.memset(zero[:], 0.0)
@@ -57,11 +58,11 @@ def tile_batchtreeencoder_kernel(tc, base, x, w_ih, b_ih, b_hh, offs, out):
         )
 
         products = {}
-        for gate in GATE_ORDER:
+        for gate in (R, NEW, Z):
             for b in range(BLOCKS):
                 products[gate, b] = psum.tile([P, N], F32, name=f"product{gate}{b}")
                 nc.tensor.matmul(
-                    products[gate, b][:], weights[gate][:, b * P : (b + 1) * P], nodes[:], start=True, stop=True
+                    products[gate, b][:], weights[:, gate * C + b : (gate + 1) * C : BLOCKS], nodes[:], start=True, stop=True
                 )
 
         reset = [held.tile([P, N], F32, name=f"reset{b}") for b in range(BLOCKS)]
@@ -83,5 +84,5 @@ def tile_batchtreeencoder_kernel(tc, base, x, w_ih, b_ih, b_hh, offs, out):
 
         for b in range(BLOCKS):
             nc.vector.tensor_tensor(windows[b][:].indirect(offsets[:]), one_minus_z[b][:], new[b][:], MULT)
-        nc.sync.dma_start(out[0:P, :], windows[0][:])
-        nc.scalar.dma_start(out[P : 2 * P, :], windows[1][:])
+        nc.sync.dma_start(out_blocks[0], windows[0][:])
+        nc.scalar.dma_start(out_blocks[1], windows[1][:])

@@ -9,6 +9,10 @@ C, E, S, N = 256, 128, 512, 128
 BLOCKS = C // P
 R, Z, NEW = 0, 1, 2
 GATES = 3
+IH, HH = 0, 1
+PIECES = GATES * BLOCKS
+SQUARE = 32
+FLIPPED = 256
 
 FLOPS = 2 * E * GATES * C * N
 
@@ -16,54 +20,46 @@ FLOPS = 2 * E * GATES * C * N
 def tile_batchtreeencoder_kernel(tc, base, x, w_ih, b_ih, b_hh, offs, out):
     nc = tc.nc
     with tc.tile_pool(name="held", bufs=1) as held, tc.psum_pool(name="psum", bufs=1) as psum:
+        bias_runs = held.tile([P, FLIPPED], F32, name="bias_runs", align_bytes=64)
+        nc.vector.memset(bias_runs[:], 0.0)
+        for s, (queue, bias) in enumerate(((nc.sync, b_ih), (nc.scalar, b_hh))):
+            queue.dma_start(
+                bias_runs[s:P:SQUARE, 0 : PIECES * SQUARE].rearrange("i (k a) -> i k a", k=PIECES),
+                bias.rearrange("(k i a) o -> i k (a o)", k=PIECES, a=SQUARE),
+            )
         nodes = held.tile([E, N], BF16, name="nodes")
-        nc.sync.dma_start(nodes[:], x)
+        nc.scalar.dma_start(nodes[:], x)
         weights = held.tile([E, GATES * C], BF16, name="weights")
         nc.sync.dma_start(weights[:], w_ih)
         offsets = held.tile([P, N // 16], U16, name="offsets")
         nc.sync.dma_start(offsets[:], offs)
-        bias_ih = held.tile([P, GATES * BLOCKS], F32, name="bias_ih")
-        bias_hh = held.tile([P, GATES * BLOCKS], F32, name="bias_hh")
-        for tile, bias in ((bias_ih, b_ih), (bias_hh, b_hh)):
-            nc.scalar.dma_start(
-                tile[:].rearrange("p (g b) -> p g b", g=GATES),
-                bias.rearrange("(g p b) o -> p g (b o)", g=GATES, b=BLOCKS),
-            )
-        base_blocks = base.rearrange("(p b) s -> b p s", b=BLOCKS)
-        out_blocks = out.rearrange("(p b) s -> b p s", b=BLOCKS)
         windows = [held.tile([P, S], F32, name=f"window{b}") for b in range(BLOCKS)]
-        nc.sync.dma_start(windows[0][:], base_blocks[0])
-        nc.scalar.dma_start(windows[1][:], base_blocks[1])
+        for b in range(BLOCKS):
+            nc.sync.dma_start(windows[b][:], base[b * P : (b + 1) * P, :])
 
         zero = held.tile([P, 1], F32, name="zero")
         nc.vector.memset(zero[:], 0.0)
         warmed = held.tile([P, 1], F32, name="warmed")
         nc.scalar.activation(warmed[:], zero[:], SIGMOID)
 
-        def column(gate, b):
-            return slice(gate * BLOCKS + b, gate * BLOCKS + b + 1)
+        biases = held.tile([P, FLIPPED], F32, name="biases", align_bytes=64)
+        nc.vector.transpose(biases[:], bias_runs[:])
+
+        def bias_of(s, gate, first_block=0, blocks=BLOCKS):
+            first = (gate * BLOCKS + first_block) * SQUARE + s
+            return biases[:, first : first + blocks * SQUARE : SQUARE]
 
         bias_r = held.tile([P, BLOCKS], F32, name="bias_r")
-        nc.vector.tensor_tensor(
-            bias_r[:], bias_ih[:, R * BLOCKS : (R + 1) * BLOCKS], bias_hh[:, R * BLOCKS : (R + 1) * BLOCKS], ADD
-        )
+        nc.vector.tensor_tensor(bias_r[:], bias_of(IH, R), bias_of(HH, R), ADD)
         minus_bias_z = held.tile([P, BLOCKS], F32, name="minus_bias_z")
-        nc.vector.scalar_tensor_tensor(
-            minus_bias_z[:],
-            bias_ih[:, Z * BLOCKS : (Z + 1) * BLOCKS],
-            -1.0,
-            bias_hh[:, Z * BLOCKS : (Z + 1) * BLOCKS],
-            MULT,
-            SUBTRACT,
-        )
+        nc.vector.scalar_tensor_tensor(minus_bias_z[:], bias_of(IH, Z), -1.0, bias_of(HH, Z), MULT, SUBTRACT)
 
         products = {}
         for gate in (R, NEW, Z):
             for b in range(BLOCKS):
                 products[gate, b] = psum.tile([P, N], F32, name=f"product{gate}{b}")
-                nc.tensor.matmul(
-                    products[gate, b][:], weights[:, gate * C + b : (gate + 1) * C : BLOCKS], nodes[:], start=True, stop=True
-                )
+                first = gate * C + b * P
+                nc.tensor.matmul(products[gate, b][:], weights[:, first : first + P], nodes[:], start=True, stop=True)
 
         reset = [held.tile([P, N], F32, name=f"reset{b}") for b in range(BLOCKS)]
         for b in range(BLOCKS):
@@ -71,7 +67,7 @@ def tile_batchtreeencoder_kernel(tc, base, x, w_ih, b_ih, b_hh, offs, out):
         before_tanh = [held.tile([P, N], F32, name=f"before_tanh{b}") for b in range(BLOCKS)]
         for b in range(BLOCKS):
             nc.vector.scalar_tensor_tensor(
-                before_tanh[b][:], reset[b][:], bias_hh[:, column(NEW, b)], products[NEW, b][:], MULT, ADD
+                before_tanh[b][:], reset[b][:], bias_of(HH, NEW, b, 1), products[NEW, b][:], MULT, ADD
             )
         one_minus_z = [held.tile([P, N], F32, name=f"one_minus_z{b}") for b in range(BLOCKS)]
         for b in range(BLOCKS):
@@ -80,9 +76,9 @@ def tile_batchtreeencoder_kernel(tc, base, x, w_ih, b_ih, b_hh, offs, out):
             )
         new = [held.tile([P, N], F32, name=f"new{b}") for b in range(BLOCKS)]
         for b in range(BLOCKS):
-            nc.scalar.activation(new[b][:], before_tanh[b][:], TANH, bias=bias_ih[:, column(NEW, b)], scale=1.0)
+            nc.scalar.activation(new[b][:], before_tanh[b][:], TANH, bias=bias_of(IH, NEW, b, 1), scale=1.0)
 
         for b in range(BLOCKS):
             nc.vector.tensor_tensor(windows[b][:].indirect(offsets[:]), one_minus_z[b][:], new[b][:], MULT)
-        nc.sync.dma_start(out_blocks[0], windows[0][:])
-        nc.scalar.dma_start(out_blocks[1], windows[1][:])
+        nc.sync.dma_start(out[0:P, :], windows[0][:])
+        nc.scalar.dma_start(out[P : 2 * P, :], windows[1][:])

@@ -9,6 +9,7 @@ C, E, S, N = 256, 128, 512, 128
 BLOCKS = C // P
 R, Z, NEW = 0, 1, 2
 GATES = 3
+GATE_ORDER = (R, NEW, Z)
 IH, HH = 0, 1
 PIECES = GATES * BLOCKS
 SQUARE = 32
@@ -29,8 +30,10 @@ def tile_batchtreeencoder_kernel(tc, base, x, w_ih, b_ih, b_hh, offs, out):
             )
         nodes = held.tile([E, N], BF16, name="nodes")
         nc.scalar.dma_start(nodes[:], x)
-        weights = held.tile([E, GATES * C], BF16, name="weights")
-        nc.sync.dma_start(weights[:], w_ih)
+        weights = {}
+        for gate in GATE_ORDER:
+            weights[gate] = held.tile([E, C], BF16, name=f"weights{gate}")
+            nc.sync.dma_start(weights[gate][:], w_ih[:, gate * C : (gate + 1) * C])
         offsets = held.tile([P, N // 16], U16, name="offsets")
         nc.sync.dma_start(offsets[:], offs)
         windows = [held.tile([P, S], F32, name=f"window{b}") for b in range(BLOCKS)]
@@ -43,7 +46,9 @@ def tile_batchtreeencoder_kernel(tc, base, x, w_ih, b_ih, b_hh, offs, out):
         nc.scalar.activation(warmed[:], zero[:], SIGMOID)
 
         biases = held.tile([P, FLIPPED], F32, name="biases", align_bytes=64)
-        nc.vector.transpose(biases[:], bias_runs[:])
+        for half in range(2):
+            columns = slice(half * FLIPPED // 2, (half + 1) * FLIPPED // 2)
+            nc.vector.transpose(biases[:, columns], bias_runs[:, columns])
 
         def bias_of(s, gate, first_block=0, blocks=BLOCKS):
             first = (gate * BLOCKS + first_block) * SQUARE + s
@@ -55,11 +60,12 @@ def tile_batchtreeencoder_kernel(tc, base, x, w_ih, b_ih, b_hh, offs, out):
         nc.vector.scalar_tensor_tensor(minus_bias_z[:], bias_of(IH, Z), -1.0, bias_of(HH, Z), MULT, SUBTRACT)
 
         products = {}
-        for gate in (R, NEW, Z):
+        for gate in GATE_ORDER:
             for b in range(BLOCKS):
                 products[gate, b] = psum.tile([P, N], F32, name=f"product{gate}{b}")
-                first = gate * C + b * P
-                nc.tensor.matmul(products[gate, b][:], weights[:, first : first + P], nodes[:], start=True, stop=True)
+                nc.tensor.matmul(
+                    products[gate, b][:], weights[gate][:, b * P : (b + 1) * P], nodes[:], start=True, stop=True
+                )
 
         reset = [held.tile([P, N], F32, name=f"reset{b}") for b in range(BLOCKS)]
         for b in range(BLOCKS):
@@ -80,5 +86,5 @@ def tile_batchtreeencoder_kernel(tc, base, x, w_ih, b_ih, b_hh, offs, out):
 
         for b in range(BLOCKS):
             nc.vector.tensor_tensor(windows[b][:].indirect(offsets[:]), one_minus_z[b][:], new[b][:], MULT)
-        nc.sync.dma_start(out[0:P, :], windows[0][:])
-        nc.scalar.dma_start(out[P : 2 * P, :], windows[1][:])
+        nc.scalar.dma_start(out[0:P, :], windows[0][:])
+        nc.sync.dma_start(out[P : 2 * P, :], windows[1][:])

@@ -22,7 +22,8 @@ def tile_batchtreeencoder_kernel(tc, base, x, w_ih, b_ih, b_hh, offs, out):
     nc = tc.nc
     with tc.tile_pool(name="held", bufs=1) as held, tc.psum_pool(name="psum", bufs=1) as psum:
         bias_runs = held.tile([P, FLIPPED], F32, name="bias_runs", align_bytes=64)
-        nc.vector.memset(bias_runs[:], 0.0)
+        nc.vector.memset(bias_runs[:, 0 : PIECES * SQUARE], 0.0)
+        nc.gpsimd.memset(bias_runs[:, PIECES * SQUARE : FLIPPED], 0.0)
         for s, (queue, bias) in enumerate(((nc.sync, b_ih), (nc.scalar, b_hh))):
             queue.dma_start(
                 bias_runs[s:P:SQUARE, 0 : PIECES * SQUARE].rearrange("i (k a) -> i k a", k=PIECES),
@@ -67,13 +68,18 @@ def tile_batchtreeencoder_kernel(tc, base, x, w_ih, b_ih, b_hh, offs, out):
                     products[gate, b][:], weights[gate][:, b * P : (b + 1) * P], nodes[:], start=True, stop=True
                 )
 
+        pieces = ((0, 0, N // 2), (0, N // 2, N // 2), (1, 0, N))
         reset = [held.tile([P, N], F32, name=f"reset{b}") for b in range(BLOCKS)]
-        for b in range(BLOCKS):
-            nc.scalar.activation(reset[b][:], products[R, b][:], SIGMOID, bias=bias_r[:, b : b + 1], scale=1.0)
+        for b, first, nodes_here in pieces:
+            here = slice(first, first + nodes_here)
+            nc.scalar.activation(
+                reset[b][:, here], products[R, b][:, here], SIGMOID, bias=bias_r[:, b : b + 1], scale=1.0
+            )
         before_tanh = [held.tile([P, N], F32, name=f"before_tanh{b}") for b in range(BLOCKS)]
-        for b in range(BLOCKS):
+        for b, first, nodes_here in pieces:
+            here = slice(first, first + nodes_here)
             nc.vector.scalar_tensor_tensor(
-                before_tanh[b][:], reset[b][:], bias_of(HH, NEW, b, 1), products[NEW, b][:], MULT, ADD
+                before_tanh[b][:, here], reset[b][:, here], bias_of(HH, NEW, b, 1), products[NEW, b][:, here], MULT, ADD
             )
         one_minus_z = [held.tile([P, N], F32, name=f"one_minus_z{b}") for b in range(BLOCKS)]
         for b in range(BLOCKS):
@@ -81,8 +87,9 @@ def tile_batchtreeencoder_kernel(tc, base, x, w_ih, b_ih, b_hh, offs, out):
                 one_minus_z[b][:], products[Z, b][:], SIGMOID, bias=minus_bias_z[:, b : b + 1], scale=-1.0
             )
         new = [held.tile([P, N], F32, name=f"new{b}") for b in range(BLOCKS)]
-        for b in range(BLOCKS):
-            nc.scalar.activation(new[b][:], before_tanh[b][:], TANH, bias=bias_of(IH, NEW, b, 1), scale=1.0)
+        for b, first, nodes_here in pieces:
+            here = slice(first, first + nodes_here)
+            nc.scalar.activation(new[b][:, here], before_tanh[b][:, here], TANH, bias=bias_of(IH, NEW, b, 1), scale=1.0)
 
         for b in range(BLOCKS):
             nc.vector.tensor_tensor(windows[b][:].indirect(offsets[:]), one_minus_z[b][:], new[b][:], MULT)

@@ -23,7 +23,7 @@ def tile_batchtreeencoder_kernel(tc, base, x, w_ih, b_ih, b_hh, offs, out):
     with tc.tile_pool(name="held", bufs=1) as held, tc.psum_pool(name="psum", bufs=1) as psum:
         bias_runs = held.tile([P, FLIPPED], F32, name="bias_runs", align_bytes=64)
         nc.vector.memset(bias_runs[:, 0 : PIECES * SQUARE], 0.0)
-        nc.gpsimd.memset(bias_runs[:, PIECES * SQUARE : FLIPPED], 0.0)
+        nc.vector.memset(bias_runs[:, PIECES * SQUARE : FLIPPED], 0.0)
         for s, (queue, bias) in enumerate(((nc.sync, b_ih), (nc.scalar, b_hh))):
             queue.dma_start(
                 bias_runs[s:P:SQUARE, 0 : PIECES * SQUARE].rearrange("i (k a) -> i k a", k=PIECES),

@@ -9,7 +9,6 @@ C, E, S, N = 256, 128, 512, 128
 BLOCKS = C // P
 R, Z, NEW = 0, 1, 2
 GATES = 3
-GATE_ORDER = (R, NEW, Z)
 IH, HH = 0, 1
 PIECES = GATES * BLOCKS
 SQUARE = 32
@@ -31,10 +30,8 @@ def tile_batchtreeencoder_kernel(tc, base, x, w_ih, b_ih, b_hh, offs, out):
             )
         nodes = held.tile([E, N], BF16, name="nodes")
         nc.scalar.dma_start(nodes[:], x)
-        weights = {}
-        for gate in GATE_ORDER:
-            weights[gate] = held.tile([E, C], BF16, name=f"weights{gate}")
-            nc.sync.dma_start(weights[gate][:], w_ih[:, gate * C : (gate + 1) * C])
+        weights = held.tile([E, GATES * C], BF16, name="weights")
+        nc.sync.dma_start(weights[:], w_ih)
         offsets = held.tile([P, N // 16], U16, name="offsets")
         nc.sync.dma_start(offsets[:], offs)
         windows = [held.tile([P, S], F32, name=f"window{b}") for b in range(BLOCKS)]
@@ -61,12 +58,11 @@ def tile_batchtreeencoder_kernel(tc, base, x, w_ih, b_ih, b_hh, offs, out):
         nc.vector.scalar_tensor_tensor(minus_bias_z[:], bias_of(IH, Z), -1.0, bias_of(HH, Z), MULT, SUBTRACT)
 
         products = {}
-        for gate in GATE_ORDER:
-            for b in range(BLOCKS):
+        for b in range(BLOCKS):
+            for gate in (R, NEW, Z):
                 products[gate, b] = psum.tile([P, N], F32, name=f"product{gate}{b}")
-                nc.tensor.matmul(
-                    products[gate, b][:], weights[gate][:, b * P : (b + 1) * P], nodes[:], start=True, stop=True
-                )
+                first = gate * C + b * P
+                nc.tensor.matmul(products[gate, b][:], weights[:, first : first + P], nodes[:], start=True, stop=True)
 
         pieces = ((0, 0, N // 2), (0, N // 2, N // 2), (1, 0, N))
         reset = [held.tile([P, N], F32, name=f"reset{b}") for b in range(BLOCKS)]

@@ -10,9 +10,9 @@ BLOCKS = C // P
 R, Z, NEW = 0, 1, 2
 GATES = 3
 IH, HH = 0, 1
-PIECES = GATES * BLOCKS
+PIECES = (GATES - 1) * BLOCKS
 SQUARE = 32
-FLIPPED = 256
+FLIPPED = PIECES * SQUARE
 
 FLOPS = 2 * E * GATES * C * N
 
@@ -20,18 +20,20 @@ FLOPS = 2 * E * GATES * C * N
 def tile_batchtreeencoder_kernel(tc, base, x, w_ih, b_ih, b_hh, offs, out):
     nc = tc.nc
     with tc.tile_pool(name="held", bufs=1) as held, tc.psum_pool(name="psum", bufs=1) as psum:
-        bias_runs = held.tile([P, FLIPPED], F32, name="bias_runs", align_bytes=64)
-        nc.vector.memset(bias_runs[:, 0 : PIECES * SQUARE], 0.0)
-        nc.vector.memset(bias_runs[:, PIECES * SQUARE : FLIPPED], 0.0)
+        r_rows = held.tile([2 * BLOCKS, P], F32, name="r_rows")
         for s, (queue, bias) in enumerate(((nc.sync, b_ih), (nc.scalar, b_hh))):
-            queue.dma_start(
-                bias_runs[s:P:SQUARE, 0 : PIECES * SQUARE].rearrange("i (k a) -> i k a", k=PIECES),
-                bias.rearrange("(k i a) o -> i k (a o)", k=PIECES, a=SQUARE),
-            )
+            queue.dma_start(r_rows[s : 2 * BLOCKS : 2, :], bias[0:C, :].rearrange("(b c) o -> b (c o)", b=BLOCKS))
         nodes = held.tile([E, N], BF16, name="nodes")
         nc.scalar.dma_start(nodes[:], x)
         weights = held.tile([E, GATES * C], BF16, name="weights")
         nc.sync.dma_start(weights[:], w_ih)
+        bias_runs = held.tile([P, FLIPPED], F32, name="bias_runs", align_bytes=64)
+        nc.vector.memset(bias_runs[:], 0.0)
+        for s, (queue, bias) in enumerate(((nc.sync, b_ih), (nc.scalar, b_hh))):
+            queue.dma_start(
+                bias_runs[s:P:SQUARE, :].rearrange("i (k a) -> i k a", k=PIECES),
+                bias[C : GATES * C, :].rearrange("(k i a) o -> i k (a o)", k=PIECES, a=SQUARE),
+            )
         offsets = held.tile([P, N // 16], U16, name="offsets")
         nc.sync.dma_start(offsets[:], offs)
         windows = [held.tile([P, S], F32, name=f"window{b}") for b in range(BLOCKS)]
@@ -43,17 +45,23 @@ def tile_batchtreeencoder_kernel(tc, base, x, w_ih, b_ih, b_hh, offs, out):
         warmed = held.tile([P, 1], F32, name="warmed")
         nc.scalar.activation(warmed[:], zero[:], SIGMOID)
 
+        pairs = held.tile([2 * BLOCKS, BLOCKS], F32, name="pairs")
+        nc.vector.memset(pairs[:, 0:1], 0.0)
+        nc.vector.memset(pairs[:, 1:2], 1.0)
+        nc.vector.memset(pairs[0:2, 0:1], 1.0)
+        nc.vector.memset(pairs[0:2, 1:2], 0.0)
+        upright_r = psum.tile([P, BLOCKS], F32, name="upright_r")
+        nc.tensor.matmul(upright_r[:], r_rows[:], pairs[:], start=True, stop=True)
+        bias_r = held.tile([P, BLOCKS], F32, name="bias_r")
+        nc.vector.tensor_copy(bias_r[:], upright_r[:])
+
         biases = held.tile([P, FLIPPED], F32, name="biases", align_bytes=64)
-        for half in range(2):
-            columns = slice(half * FLIPPED // 2, (half + 1) * FLIPPED // 2)
-            nc.vector.transpose(biases[:, columns], bias_runs[:, columns])
+        nc.vector.transpose(biases[:], bias_runs[:])
 
         def bias_of(s, gate, first_block=0, blocks=BLOCKS):
-            first = (gate * BLOCKS + first_block) * SQUARE + s
-            return biases[:, first : first + blocks * SQUARE : SQUARE]
+            first = ((gate - 1) * BLOCKS + first_block) * SQUARE + s
+            return biases[:, first : first + (blocks - 1) * SQUARE + 1 : SQUARE]
 
-        bias_r = held.tile([P, BLOCKS], F32, name="bias_r")
-        nc.vector.tensor_tensor(bias_r[:], bias_of(IH, R), bias_of(HH, R), ADD)
         minus_bias_z = held.tile([P, BLOCKS], F32, name="minus_bias_z")
         nc.vector.scalar_tensor_tensor(minus_bias_z[:], bias_of(IH, Z), -1.0, bias_of(HH, Z), MULT, SUBTRACT)
 

import concourse.mybir as mybir

F32, BF16, U16 = mybir.dt.float32, mybir.dt.bfloat16, mybir.dt.uint16
MULT, ADD, SUBTRACT = mybir.AluOpType.mult, mybir.AluOpType.add, mybir.AluOpType.subtract
SIGMOID, TANH = mybir.ActivationFunctionType.Sigmoid, mybir.ActivationFunctionType.Tanh

P = 128
C, E, S, N = 256, 128, 512, 128
BLOCKS = C // P
R, Z, NEW = 0, 1, 2
GATES = 3
IH, HH = 0, 1
PIECES = (GATES - 1) * BLOCKS
SQUARE = 32
FLIPPED = PIECES * SQUARE

FLOPS = 2 * E * GATES * C * N


def tile_batchtreeencoder_kernel(tc, base, x, w_ih, b_ih, b_hh, offs, out):
    nc = tc.nc
    with tc.tile_pool(name="held", bufs=1) as held, tc.psum_pool(name="psum", bufs=1) as psum:
        r_rows = held.tile([2 * BLOCKS, P], F32, name="r_rows")
        for s, (queue, bias) in enumerate(((nc.sync, b_ih), (nc.scalar, b_hh))):
            queue.dma_start(r_rows[s : 2 * BLOCKS : 2, :], bias[0:C, :].rearrange("(b c) o -> b (c o)", b=BLOCKS))
        nodes = held.tile([E, N], BF16, name="nodes")
        nc.scalar.dma_start(nodes[:], x)
        weights = held.tile([E, GATES * C], BF16, name="weights")
        nc.sync.dma_start(weights[:], w_ih)
        bias_runs = held.tile([P, FLIPPED], F32, name="bias_runs", align_bytes=64)
        nc.vector.memset(bias_runs[:], 0.0)
        for s, (queue, bias) in enumerate(((nc.sync, b_ih), (nc.scalar, b_hh))):
            queue.dma_start(
                bias_runs[s:P:SQUARE, :].rearrange("i (k a) -> i k a", k=PIECES),
                bias[C : GATES * C, :].rearrange("(k i a) o -> i k (a o)", k=PIECES, a=SQUARE),
            )
        offsets = held.tile([P, N // 16], U16, name="offsets")
        nc.sync.dma_start(offsets[:], offs)
        windows = [held.tile([P, S], F32, name=f"window{b}") for b in range(BLOCKS)]
        for b in range(BLOCKS):
            nc.sync.dma_start(windows[b][:], base[b * P : (b + 1) * P, :])

        zero = held.tile([P, 1], F32, name="zero")
        nc.vector.memset(zero[:], 0.0)
        warmed = held.tile([P, 1], F32, name="warmed")
        nc.scalar.activation(warmed[:], zero[:], SIGMOID)

        pairs = held.tile([2 * BLOCKS, BLOCKS], F32, name="pairs")
        nc.vector.memset(pairs[:, 0:1], 0.0)
        nc.vector.memset(pairs[:, 1:2], 1.0)
        nc.vector.memset(pairs[0:2, 0:1], 1.0)
        nc.vector.memset(pairs[0:2, 1:2], 0.0)
        upright_r = psum.tile([P, BLOCKS], F32, name="upright_r")
        nc.tensor.matmul(upright_r[:], r_rows[:], pairs[:], start=True, stop=True)
        bias_r = held.tile([P, BLOCKS], F32, name="bias_r")
        nc.vector.tensor_copy(bias_r[:], upright_r[:])

        biases = held.tile([P, FLIPPED], F32, name="biases", align_bytes=64)
        nc.vector.transpose(biases[:], bias_runs[:])

        def bias_of(s, gate, first_block=0, blocks=BLOCKS):
            first = ((gate - 1) * BLOCKS + first_block) * SQUARE + s
            return biases[:, first : first + (blocks - 1) * SQUARE + 1 : SQUARE]

        minus_bias_z = held.tile([P, BLOCKS], F32, name="minus_bias_z")
        nc.vector.scalar_tensor_tensor(minus_bias_z[:], bias_of(IH, Z), -1.0, bias_of(HH, Z), MULT, SUBTRACT)

        products = {}
        for b in range(BLOCKS):
            for gate in (R, NEW, Z):
                products[gate, b] = psum.tile([P, N], F32, name=f"product{gate}{b}")
                first = gate * C + b * P
                nc.tensor.matmul(products[gate, b][:], weights[:, first : first + P], nodes[:], start=True, stop=True)

        pieces = ((0, 0, N // 2), (0, N // 2, N // 2), (1, 0, N))
        reset = [held.tile([P, N], F32, name=f"reset{b}") for b in range(BLOCKS)]
        for b, first, nodes_here in pieces:
            here = slice(first, first + nodes_here)
            nc.scalar.activation(
                reset[b][:, here], products[R, b][:, here], SIGMOID, bias=bias_r[:, b : b + 1], scale=1.0
            )
        before_tanh = [held.tile([P, N], F32, name=f"before_tanh{b}") for b in range(BLOCKS)]
        for b, first, nodes_here in pieces:
            here = slice(first, first + nodes_here)
            nc.vector.scalar_tensor_tensor(
                before_tanh[b][:, here], reset[b][:, here], bias_of(HH, NEW, b, 1), products[NEW, b][:, here], MULT, ADD
            )
        one_minus_z = [held.tile([P, N], F32, name=f"one_minus_z{b}") for b in range(BLOCKS)]
        for b in range(BLOCKS):
            nc.scalar.activation(
                one_minus_z[b][:], products[Z, b][:], SIGMOID, bias=minus_bias_z[:, b : b + 1], scale=-1.0
            )
        new = [held.tile([P, N], F32, name=f"new{b}") for b in range(BLOCKS)]
        for b, first, nodes_here in pieces:
            here = slice(first, first + nodes_here)
            nc.scalar.activation(new[b][:, here], before_tanh[b][:, here], TANH, bias=bias_of(IH, NEW, b, 1), scale=1.0)

        for b in range(BLOCKS):
            nc.vector.tensor_tensor(windows[b][:].indirect(offsets[:]), one_minus_z[b][:], new[b][:], MULT)
        nc.scalar.dma_start(out[0:P, :], windows[0][:])
        nc.sync.dma_start(out[P : 2 * P, :], windows[1][:])
